import numpy as np
import ml_dtypes

BF16 = ml_dtypes.bfloat16


def bf(x):
    return np.asarray(x, np.float32).astype(BF16)


def f32(x):
    return np.asarray(x, np.float32)


def f64(x):
    return np.asarray(x).astype(np.float64)


def striped(idx):
    return np.tile(idx.reshape(-1, 16).T, (8, 1))


IQ, OQ, K, C, S, N = 128, 32, 512, 128, 256, 128
LIM = np.sqrt(6.0 / (IQ + OQ))


def draw_w():
    return bf(np.random.uniform(-LIM, LIM, (IQ, OQ)))


def setup_inputs():
    return {"base": f32(np.random.standard_normal((C, S))), "x": bf(np.random.standard_normal((K, N))), "wr": draw_w(), "wi": draw_w(), "wj": draw_w(), "wk": draw_w(), "bias": f32(0.1 * np.random.standard_normal((C, 1))), "offs": striped(np.random.permutation(S)[:N])}


def reference(base, x, wr, wi, wj, wk, bias, offs):
    idx = offs[:16].T.reshape(-1)
    r, i, j, k = f64(wr), f64(wi), f64(wj), f64(wk)
    big = np.block([[r, i, j, k], [-i, r, i, -i], [-j, -j, r, j], [-k, k, -k, r]])
    out = f64(base).copy()
    out[:, idx] = big.T @ f64(x) + f64(bias)
    return out

@@ -1,0 +1,68 @@
+import concourse.mybir as mybir
+
+F32 = mybir.dt.float32
+BF16 = mybir.dt.bfloat16
+U16 = mybir.dt.uint16
+ADD = mybir.AluOpType.add
+
+P = 128
+OQ = 32
+N = 128
+S = 256
+FLOPS = 2 * 4 * P * P * N
+
+BLOCKS = (
+    ("+r", "+i", "+j", "+k"),
+    ("-i", "+r", "+i", "-i"),
+    ("-j", "-j", "+r", "+j"),
+    ("-k", "+k", "-k", "+r"),
+)
+
+
+def tile_quaternionlinear_kernel(tc, base, x, wr, wi, wj, wk, bias, offs, out):
+    nc = tc.nc
+    with (
+        tc.tile_pool(name="held", bufs=1) as held,
+        tc.psum_pool(name="psum", bufs=1) as psum,
+    ):
+        big = [held.tile([P, 4, OQ], BF16, name=f"big{q}") for q in range(4)]
+        column_of = {}
+        for c, (letter, w) in enumerate((("r", wr), ("i", wi), ("j", wj), ("k", wk))):
+            column_of[letter] = c
+            nc.sync.dma_start(big[0][:, c, :], w)
+
+        xq = held.tile([P, 4, N], BF16, name="xq")
+        nc.scalar.dma_start(xq[:], x.rearrange("(q k) j -> k q j", k=P))
+
+        offsets = held.tile([P, N // 16], U16, name="offsets")
+        nc.sync.dma_start(offsets[:], offs)
+
+        bias_col = held.tile([P, 1], F32, name="bias_col")
+        nc.scalar.dma_start(bias_col[:], bias)
+        window = held.tile([P, S], F32, name="window")
+        nc.gpsimd.dma_start(window[:], base)
+        bias_wide = held.tile([P, N], F32, name="bias_wide")
+        nc.gpsimd.tensor_copy(bias_wide[:], bias_col[:, 0:1].to_broadcast([P, N]))
+
+        for q in range(1, 4):
+            nc.vector.tensor_copy(big[q][:, BLOCKS[q].index("+r"), :], big[0][:, column_of["r"], :])
+        for q in range(1, 4):
+            plus = [c for c in range(4) if BLOCKS[q][c][0] == "+" and BLOCKS[q][c] != "+r"]
+            minus = [c for c in range(4) if BLOCKS[q][c][0] == "-"]
+            letter = BLOCKS[q][minus[0]][1]
+            source = big[0][:, column_of[letter] : column_of[letter] + 1, :]
+            both = big[q][:, minus[0] : minus[1] + 1 : minus[1] - minus[0], :]
+            nc.vector.tensor_scalar_mul(both, source.to_broadcast([P, 2, OQ]), -1.0)
+            nc.vector.tensor_copy(big[q][:, plus[0] : plus[0] + 1, :], source)
+
+        y = psum.tile([P, N], F32, name="y")
+        for q in range(4):
+            nc.tensor.matmul(
+                y[:], big[q][:].rearrange("k c o -> k (c o)"), xq[:, q, :], start=(q == 0), stop=(q == 3)
+            )
+
+        y_sbuf = held.tile([P, N], F32, name="y_sbuf")
+        nc.vector.tensor_copy(y_sbuf[:], y[:])
+
+        nc.vector.tensor_tensor(window[:].indirect(offsets[:]), y_sbuf[:], bias_wide[:], ADD)
+        nc.sync.dma_start(out, window[:])

@@ -27,12 +27,13 @@ def tile_quaternionlinear_kernel(tc, base, x, wr, wi, wj, wk, bias, offs, out):
     ):
         big = [held.tile([P, 4, OQ], BF16, name=f"big{q}") for q in range(4)]
         column_of = {}
-        for c, (letter, w) in enumerate((("r", wr), ("i", wi), ("j", wj), ("k", wk))):
-            column_of[letter] = c
-            nc.sync.dma_start(big[0][:, c, :], w)
 
         xq = held.tile([P, 4, N], BF16, name="xq")
-        nc.scalar.dma_start(xq[:], x.rearrange("(q k) j -> k q j", k=P))
+        nc.sync.dma_start(xq[:], x.rearrange("(q k) j -> k q j", k=P))
+        for c, (letter, w) in enumerate((("r", wr), ("i", wi), ("j", wj), ("k", wk))):
+            column_of[letter] = c
+            queue = nc.sync if c % 2 == 0 else nc.scalar
+            queue.dma_start(big[0][:, c, :], w)
 
         offsets = held.tile([P, N // 16], U16, name="offsets")
         nc.sync.dma_start(offsets[:], offs)

@@ -39,7 +39,7 @@ def tile_quaternionlinear_kernel(tc, base, x, wr, wi, wj, wk, bias, offs, out):
         nc.sync.dma_start(offsets[:], offs)
 
         bias_col = held.tile([P, 1], F32, name="bias_col")
-        nc.scalar.dma_start(bias_col[:], bias)
+        nc.sync.dma_start(bias_col[:], bias)
         window = held.tile([P, S], F32, name="window")
         nc.gpsimd.dma_start(window[:], base)
         bias_wide = held.tile([P, N], F32, name="bias_wide")

@@ -29,10 +29,10 @@ def tile_quaternionlinear_kernel(tc, base, x, wr, wi, wj, wk, bias, offs, out):
         column_of = {}
 
         xq = held.tile([P, 4, N], BF16, name="xq")
-        nc.sync.dma_start(xq[:], x.rearrange("(q k) j -> k q j", k=P))
+        nc.scalar.dma_start(xq[:], x.rearrange("(q k) j -> k q j", k=P))
         for c, (letter, w) in enumerate((("r", wr), ("i", wi), ("j", wj), ("k", wk))):
             column_of[letter] = c
-            queue = nc.sync if c % 2 == 0 else nc.scalar
+            queue = nc.scalar if letter == "k" else nc.sync
             queue.dma_start(big[0][:, c, :], w)
 
         offsets = held.tile([P, N // 16], U16, name="offsets")

import concourse.mybir as mybir

F32 = mybir.dt.float32
BF16 = mybir.dt.bfloat16
U16 = mybir.dt.uint16
ADD = mybir.AluOpType.add

P = 128
OQ = 32
N = 128
S = 256
FLOPS = 2 * 4 * P * P * N

BLOCKS = (
    ("+r", "+i", "+j", "+k"),
    ("-i", "+r", "+i", "-i"),
    ("-j", "-j", "+r", "+j"),
    ("-k", "+k", "-k", "+r"),
)


def tile_quaternionlinear_kernel(tc, base, x, wr, wi, wj, wk, bias, offs, out):
    nc = tc.nc
    with (
        tc.tile_pool(name="held", bufs=1) as held,
        tc.psum_pool(name="psum", bufs=1) as psum,
    ):
        big = [held.tile([P, 4, OQ], BF16, name=f"big{q}") for q in range(4)]
        column_of = {}

        xq = held.tile([P, 4, N], BF16, name="xq")
        nc.scalar.dma_start(xq[:], x.rearrange("(q k) j -> k q j", k=P))
        for c, (letter, w) in enumerate((("r", wr), ("i", wi), ("j", wj), ("k", wk))):
            column_of[letter] = c
            queue = nc.scalar if letter == "k" else nc.sync
            queue.dma_start(big[0][:, c, :], w)

        offsets = held.tile([P, N // 16], U16, name="offsets")
        nc.sync.dma_start(offsets[:], offs)

        bias_col = held.tile([P, 1], F32, name="bias_col")
        nc.sync.dma_start(bias_col[:], bias)
        window = held.tile([P, S], F32, name="window")
        nc.gpsimd.dma_start(window[:], base)
        bias_wide = held.tile([P, N], F32, name="bias_wide")
        nc.gpsimd.tensor_copy(bias_wide[:], bias_col[:, 0:1].to_broadcast([P, N]))

        for q in range(1, 4):
            nc.vector.tensor_copy(big[q][:, BLOCKS[q].index("+r"), :], big[0][:, column_of["r"], :])
        for q in range(1, 4):
            plus = [c for c in range(4) if BLOCKS[q][c][0] == "+" and BLOCKS[q][c] != "+r"]
            minus = [c for c in range(4) if BLOCKS[q][c][0] == "-"]
            letter = BLOCKS[q][minus[0]][1]
            source = big[0][:, column_of[letter] : column_of[letter] + 1, :]
            both = big[q][:, minus[0] : minus[1] + 1 : minus[1] - minus[0], :]
            nc.vector.tensor_scalar_mul(both, source.to_broadcast([P, 2, OQ]), -1.0)
            nc.vector.tensor_copy(big[q][:, plus[0] : plus[0] + 1, :], source)

        y = psum.tile([P, N], F32, name="y")
        for q in range(4):
            nc.tensor.matmul(
                y[:], big[q][:].rearrange("k c o -> k (c o)"), xq[:, q, :], start=(q == 0), stop=(q == 3)
            )

        y_sbuf = held.tile([P, N], F32, name="y_sbuf")
        nc.vector.tensor_copy(y_sbuf[:], y[:])

        nc.vector.tensor_tensor(window[:].indirect(offsets[:]), y_sbuf[:], bias_wide[:], ADD)
        nc.sync.dma_start(out, window[:])
